import numpy as np
import ml_dtypes


def mxq(x, axis, fmt="e4m3"):
    dtype, down = {"e4m3": (ml_dtypes.float8_e4m3fn, 7), "e5m2": (ml_dtypes.float8_e5m2, 14)}[fmt]
    v = np.moveaxis(np.asarray(x, np.float32).astype(ml_dtypes.bfloat16).astype(np.float64), axis, -1)
    blocks = v.reshape(v.shape[:-1] + (-1, 32))
    amax = np.abs(blocks).max(-1, keepdims=True)
    byte = np.maximum(np.where(amax > 0, np.frexp(amax)[1] - 1 + 127, 0) - down, 1)
    scale = np.exp2(byte - 127.0)
    codes = (blocks / scale).astype(np.float32).astype(dtype).astype(np.float64)
    return np.moveaxis((codes * scale).reshape(v.shape), -1, axis)


WIDE = False


def mx_kscale(k):
    if not WIDE:
        return np.ones(k)
    levels = np.array([10, -10, 5, -5, 0])
    a = np.random.permutation(np.resize(levels, k // 512 * 4)).reshape(k // 512, 4)
    idx = np.arange(k)
    return np.exp2(a[idx // 512, idx % 128 // 32])


BF16 = ml_dtypes.bfloat16


def bf(x):
    return np.asarray(x, np.float32).astype(BF16)


def f64(x):
    return np.asarray(x).astype(np.float64)


E2M1 = np.array([0.0, 0.5, 1.0, 1.5, 2.0, 3.0, 4.0, 6.0, -0.0, -0.5, -1.0, -1.5, -2.0, -3.0, -4.0, -6.0])


def pack_weight(w, fmt):
    k, n = w.shape
    w = f64(bf(w)).reshape(k // 32, 32, n)
    amax = np.abs(w).max(1)
    if fmt == "e4m3":
        byte = np.frexp(amax)[1] - 1 + 127 - 7
    else:
        mant, ex = np.frexp(amax / 6.0)
        byte = np.where(mant > 0.5, ex, ex - 1) + 127
    byte = np.clip(np.where(amax > 0, byte, 1), 1, 254)
    scaled = (w * np.exp2(127.0 - byte)[:, None, :]).reshape(k, n).astype(np.float32)
    by_word = np.ascontiguousarray(scaled.reshape(k // 512, 128, 4, n).transpose(0, 1, 3, 2))
    if fmt == "e4m3":
        words = by_word.astype(ml_dtypes.float8_e4m3fn).view(np.uint8)
    else:
        c = by_word.astype(ml_dtypes.float4_e2m1fn).view(np.uint8) & 0xF
        words = c[..., 0::2] | (c[..., 1::2] << 4)
    return np.ascontiguousarray(words), np.ascontiguousarray(byte.astype(np.uint8).reshape(k // 512, 16, n))


def unpack_weight(words, scales, fmt):
    g, p, n, _ = words.shape
    if fmt == "e4m3":
        vals = np.ascontiguousarray(words).view(ml_dtypes.float8_e4m3fn).astype(np.float64)
    else:
        nib = np.empty((g, p, n, 4), np.uint8)
        nib[..., 0::2] = words & 0xF
        nib[..., 1::2] = words >> 4
        vals = E2M1[nib]
    vals = vals * np.repeat(np.exp2(scales.astype(np.float64) - 127.0), 8, axis=1)[..., None]
    return vals.transpose(0, 1, 3, 2).reshape(g * 512, n)


B, T, L, D, K = 8, 1024, 256, 1024, 256
HS = 0.25
FMT = "e4m3"


def sigmoid(v):
    return 1.0 / (1.0 + np.exp(-v))


def setup_inputs():
    s = mx_kscale(D)
    H = bf(np.random.standard_normal((B, T, D)) * HS * s)
    Wr = np.random.standard_normal((K, D)) / (HS * np.sqrt(D)) / s
    words, scales = pack_weight(np.ascontiguousarray(Wr.T), FMT)
    br = bf(np.random.standard_normal(K) * 0.3)
    return {"H": H, "Wr_words": words, "Wr_scales": scales, "br": br}


def reference(H, Wr_words, Wr_scales, br):
    h = f64(H)
    route = sigmoid((mxq(h, 2, "e4m3") @ unpack_weight(Wr_words, Wr_scales, FMT)) + f64(br))
    return mxq(route, 1, "e4m3").transpose(0, 2, 1) @ mxq(h, 1, "e4m3")

@@ -1,0 +1,228 @@
+from contextlib import ExitStack
+
+import concourse.mybir as mybir
+from concourse.masks import make_identity
+
+F32 = mybir.dt.float32
+BF16 = mybir.dt.bfloat16
+I32 = mybir.dt.int32
+U32 = mybir.dt.uint32
+U8 = mybir.dt.uint8
+FP8X4 = mybir.dt.float8_e4m3fn_x4
+ADD = mybir.AluOpType.add
+SIGMOID = mybir.ActivationFunctionType.Sigmoid
+
+SEQS, FRAMES, FEATURES, SLOTS = 8, 1024, 1024, 256
+
+P = 128
+PACK = 4
+K_PASS = P * PACK
+BANK = 512
+
+CHUNK = K_PASS
+CHUNKS_PER_SEQ = FRAMES // CHUNK
+N_CHUNKS = SEQS * CHUNKS_PER_SEQ
+FEATURE_PASSES = FEATURES // K_PASS
+WORDS_PER_PASS = K_PASS // 2
+SLOT_TILES = SLOTS // P
+FEATURE_BANKS = FEATURES // BANK
+N_OUT_TILES = SEQS * SLOT_TILES
+assert N_OUT_TILES == N_CHUNKS
+
+VECTOR_FEATURES = FEATURES * 3 // 4
+
+PREFETCH = 4
+
+FLOPS = 2 * 2 * SEQS * FRAMES * FEATURES * SLOTS
+
+
+def tile_instrumentspecificslotmemory_pa_t_kernel(tc, H, Wr_words, Wr_scales, br, out):
+    nc = tc.nc
+    with ExitStack() as stack:
+        const = stack.enter_context(tc.tile_pool(name="const", bufs=1))
+        rows_pool = stack.enter_context(tc.tile_pool(name="rows", bufs=PREFETCH + 2))
+        work = stack.enter_context(tc.tile_pool(name="work", bufs=2))
+        seq_pool = stack.enter_context(tc.tile_pool(name="seq", bufs=3))
+        out_pool = stack.enter_context(tc.tile_pool(name="out", bufs=3))
+        psum_t = stack.enter_context(tc.psum_pool(name="psum_t", bufs=4))
+        psum_r = stack.enter_context(tc.psum_pool(name="psum_r", bufs=2))
+        psum_a = stack.enter_context(tc.psum_pool(name="psum_a", bufs=2))
+        stack.enter_context(tc.manual_schedule())
+
+        h_rows, h_grouped, ht_grouped, ht_codes, ht_scales, route_grouped = {}, {}, {}, {}, {}, {}
+        h_codes, h_scales, route_codes, route_scales = {}, {}, {}, {}
+        agg_banks = {}
+
+        def load(k):
+            seq, part = divmod(k, CHUNKS_PER_SEQ)
+            rows = rows_pool.tile([P, PACK, FEATURES], BF16)
+            frames = H[seq, part * CHUNK : (part + 1) * CHUNK, :]
+            nc.sync.dma_start(out=rows[:], in_=frames.rearrange("(p j) d -> p j d", j=PACK))
+            h_rows[k] = rows
+
+        load(0)
+
+        w_words = const.tile([P, FEATURE_PASSES, SLOTS], U32, align_bytes=64)
+        nc.sync.dma_start(
+            out=w_words[:].bitcast(I32),
+            in_=Wr_words.rearrange("g p n t -> p g (n t)").bitcast(I32),
+        )
+        w_scales = const.tile([P, FEATURE_PASSES, SLOTS], U8, align_bytes=64)
+        nc.vector.memset(w_scales[:].bitcast(I32), 0)
+        for quadrant in range(4):
+            nc.sync.dma_start(
+                out=w_scales[32 * quadrant : 32 * quadrant + 4, :, :].bitcast(I32),
+                in_=Wr_scales[:, 4 * quadrant : 4 * quadrant + 4, :].rearrange("g r n -> r g n").bitcast(I32),
+            )
+        for k in range(1, PREFETCH):
+            load(k)
+
+        bias = const.tile([P, SLOTS], BF16)
+        nc.scalar.dma_start(out=bias[:], in_=br.partition_broadcast(P))
+
+        identity = const.tile([P, P], F32)
+        make_identity(nc, identity[:])
+
+        warm_in = const.tile([P, 1], F32)
+        warm_out = const.tile([P, 1], F32)
+        nc.vector.memset(warm_in[:], 0.0)
+        nc.scalar.activation(out=warm_out[:], in_=warm_in[:], func=SIGMOID)
+
+        def regroup(k):
+            rows = h_rows[k]
+            grouped = work.tile([P, FEATURES, PACK], BF16, align_bytes=64, name="h_grouped")
+            nc.vector.tensor_copy(
+                out=grouped[:, :VECTOR_FEATURES, :].rearrange("p (c i) j -> p c j i", i=4),
+                in_=rows[:, :, :VECTOR_FEATURES].rearrange("p j (c i) -> p c j i", i=4),
+            )
+            nc.scalar.copy(
+                out=grouped[:, VECTOR_FEATURES:, :].rearrange("p (c i) j -> p c j i", i=4),
+                in_=rows[:, :, VECTOR_FEATURES:].rearrange("p j (c i) -> p c j i", i=4),
+            )
+            h_grouped[k] = grouped
+
+        def transpose(k):
+            words = h_rows[k][:].bitcast(F32)
+            grouped = work.tile([P, PACK, FEATURE_PASSES * P * PACK], BF16, align_bytes=64, name="ht_grouped")
+            for j in range(PACK):
+                bank = psum_t.tile([P, 2, FEATURE_PASSES * P], F32, name="ht_bank")
+                for g in range(FEATURE_PASSES):
+                    for u in range(2):
+                        nc.tensor.transpose(
+                            bank[:, u, g * P : (g + 1) * P],
+                            words[:, j, g * WORDS_PER_PASS + u : (g + 1) * WORDS_PER_PASS : 2],
+                            identity[:],
+                        )
+                nc.scalar.copy(
+                    out=grouped[:].bitcast(F32)[:, j, :].rearrange("p (c u) -> p c u", u=2),
+                    in_=bank[:].rearrange("p u c -> p c u"),
+                )
+            ht_grouped[k] = grouped
+
+        def quantise_h(k):
+            seq, part = divmod(k, CHUNKS_PER_SEQ)
+            if part == 0:
+                h_codes[seq] = seq_pool.tile([P, CHUNKS_PER_SEQ, FEATURES], U32, align_bytes=64, name="h_codes")
+                h_scales[seq] = seq_pool.tile([P, CHUNKS_PER_SEQ, FEATURES], U8, align_bytes=64, name="h_scales")
+            nc.vector.quantize_mx(
+                out=h_codes[seq][:, part, :].bitcast(FP8X4),
+                scales=h_scales[seq][:, part, :],
+                in_=h_grouped[k][:].rearrange("p d j -> p (d j)"),
+            )
+
+        def quantise_ht(k):
+            codes = work.tile([P, PACK, FEATURE_PASSES, P], U32, align_bytes=64, name="ht_codes")
+            scales = work.tile([P, PACK, FEATURE_PASSES, P], U8, align_bytes=64, name="ht_scales")
+            nc.vector.quantize_mx(
+                out=codes[:].rearrange("p j g c -> p (j g c)").bitcast(FP8X4),
+                scales=scales[:].rearrange("p j g c -> p (j g c)"),
+                in_=ht_grouped[k][:].rearrange("p j c -> p (j c)"),
+            )
+            ht_codes[k], ht_scales[k] = codes, scales
+
+        def route_chunk(k):
+            codes, scales = ht_codes[k], ht_scales[k]
+            logits = work.tile([P, SLOTS, PACK], F32, name="logits")
+            for s in range(SLOT_TILES):
+                slots = slice(s * P, (s + 1) * P)
+                bank = psum_r.tile([P, PACK, P], F32, name="route_bank")
+                for j in range(PACK):
+                    for g in range(FEATURE_PASSES):
+                        nc.tensor.matmul_mx(
+                            out=bank[:, j, :],
+                            lhsT=codes[:, j, g, :].bitcast(FP8X4),
+                            lhsT_scale=scales[:, j, g, :],
+                            rhs=w_words[:, g, slots].bitcast(FP8X4),
+                            rhs_scale=w_scales[:, g, slots],
+                            start=(g == 0),
+                            stop=(g == FEATURE_PASSES - 1),
+                        )
+                nc.vector.tensor_tensor(
+                    out=logits[:, slots, :],
+                    in0=bank[:].rearrange("p j n -> p n j"),
+                    in1=bias[:, slots].unsqueeze(2).to_broadcast([P, P, PACK]),
+                    op=ADD,
+                )
+            grouped = work.tile([P, SLOTS * PACK], BF16, align_bytes=64, name="route_grouped")
+            nc.scalar.activation(out=grouped[:], in_=logits[:].rearrange("p n j -> p (n j)"), func=SIGMOID)
+            route_grouped[k] = grouped
+
+        def quantise_route(k):
+            seq, part = divmod(k, CHUNKS_PER_SEQ)
+            if part == 0:
+                route_codes[seq] = seq_pool.tile([P, CHUNKS_PER_SEQ, SLOTS], U32, align_bytes=64, name="route_codes")
+                route_scales[seq] = seq_pool.tile([P, CHUNKS_PER_SEQ, SLOTS], U8, align_bytes=64, name="route_scales")
+            nc.vector.quantize_mx(
+                out=route_codes[seq][:, part, :].bitcast(FP8X4),
+                scales=route_scales[seq][:, part, :],
+                in_=route_grouped[k][:],
+            )
+
+        def aggregate(t):
+            seq, s = divmod(t, SLOT_TILES)
+            slots = slice(s * P, (s + 1) * P)
+            agg_banks[t] = []
+            for f in range(FEATURE_BANKS):
+                features = slice(f * BANK, (f + 1) * BANK)
+                bank = psum_a.tile([P, BANK], F32, name="agg_bank")
+                for part in range(CHUNKS_PER_SEQ):
+                    nc.tensor.matmul_mx(
+                        out=bank[:],
+                        lhsT=route_codes[seq][:, part, slots].bitcast(FP8X4),
+                        lhsT_scale=route_scales[seq][:, part, slots],
+                        rhs=h_codes[seq][:, part, features].bitcast(FP8X4),
+                        rhs_scale=h_scales[seq][:, part, features],
+                        start=(part == 0),
+                        stop=(part == CHUNKS_PER_SEQ - 1),
+                    )
+                agg_banks[t].append(bank)
+
+        def drain_agg(t):
+            seq, s = divmod(t, SLOT_TILES)
+            result = out_pool.tile([P, FEATURES], F32)
+            for f, bank in enumerate(agg_banks[t]):
+                nc.scalar.copy(out=result[:, f * BANK : (f + 1) * BANK], in_=bank[:])
+            nc.sync.dma_start(out=out[seq, s * P : (s + 1) * P, :], in_=result[:])
+
+        def is_chunk(i):
+            return 0 <= i < N_CHUNKS
+
+        for k in range(N_CHUNKS + 4):
+            if is_chunk(k + PREFETCH):
+                load(k + PREFETCH)
+            if is_chunk(k - 2):
+                quantise_route(k - 2)
+            if is_chunk(k - 1):
+                quantise_ht(k - 1)
+            if is_chunk(k):
+                regroup(k)
+            if is_chunk(k - 4):
+                drain_agg(k - 4)
+            if is_chunk(k):
+                transpose(k)
+            if is_chunk(k - 1):
+                route_chunk(k - 1)
+            if is_chunk(k):
+                quantise_h(k)
+            if is_chunk(k - 3):
+                aggregate(k - 3)

@@ -40,7 +40,7 @@ def tile_instrumentspecificslotmemory_pa_t_kernel(tc, H, Wr_words, Wr_scales, br
     nc = tc.nc
     with ExitStack() as stack:
         const = stack.enter_context(tc.tile_pool(name="const", bufs=1))
-        rows_pool = stack.enter_context(tc.tile_pool(name="rows", bufs=PREFETCH + 2))
+        rows_pool = stack.enter_context(tc.tile_pool(name="rows", bufs=PREFETCH + 3))
         work = stack.enter_context(tc.tile_pool(name="work", bufs=2))
         seq_pool = stack.enter_context(tc.tile_pool(name="seq", bufs=3))
         out_pool = stack.enter_context(tc.tile_pool(name="out", bufs=3))
@@ -49,7 +49,7 @@ def tile_instrumentspecificslotmemory_pa_t_kernel(tc, H, Wr_words, Wr_scales, br
         psum_a = stack.enter_context(tc.psum_pool(name="psum_a", bufs=2))
         stack.enter_context(tc.manual_schedule())
 
-        h_rows, h_grouped, ht_grouped, ht_codes, ht_scales, route_grouped = {}, {}, {}, {}, {}, {}
+        h_rows, h_grouped, ht_grouped, ht_codes, ht_scales, logits, route_grouped = {}, {}, {}, {}, {}, {}, {}
         h_codes, h_scales, route_codes, route_scales = {}, {}, {}, {}
         agg_banks = {}
 
@@ -88,23 +88,24 @@ def tile_instrumentspecificslotmemory_pa_t_kernel(tc, H, Wr_words, Wr_scales, br
         nc.vector.memset(warm_in[:], 0.0)
         nc.scalar.activation(out=warm_out[:], in_=warm_in[:], func=SIGMOID)
 
-        def regroup(k):
-            rows = h_rows[k]
-            grouped = work.tile([P, FEATURES, PACK], BF16, align_bytes=64, name="h_grouped")
+        def regroup_on_vector(k):
+            h_grouped[k] = work.tile([P, FEATURES, PACK], BF16, align_bytes=64, name="h_grouped")
             nc.vector.tensor_copy(
-                out=grouped[:, :VECTOR_FEATURES, :].rearrange("p (c i) j -> p c j i", i=4),
-                in_=rows[:, :, :VECTOR_FEATURES].rearrange("p j (c i) -> p c j i", i=4),
+                out=h_grouped[k][:, :VECTOR_FEATURES, :].rearrange("p (c i) j -> p c j i", i=4),
+                in_=h_rows[k][:, :, :VECTOR_FEATURES].rearrange("p j (c i) -> p c j i", i=4),
             )
-            nc.scalar.copy(
-                out=grouped[:, VECTOR_FEATURES:, :].rearrange("p (c i) j -> p c j i", i=4),
-                in_=rows[:, :, VECTOR_FEATURES:].rearrange("p j (c i) -> p c j i", i=4),
-            )
-            h_grouped[k] = grouped
 
-        def transpose(k):
+        def regroup_on_scalar(k):
+            nc.scalar.copy(
+                out=h_grouped[k][:, VECTOR_FEATURES:, :].rearrange("p (c i) j -> p c j i", i=4),
+                in_=h_rows[k][:, :, VECTOR_FEATURES:].rearrange("p j (c i) -> p c j i", i=4),
+            )
+
+        def transpose(k, frame_rows):
             words = h_rows[k][:].bitcast(F32)
-            grouped = work.tile([P, PACK, FEATURE_PASSES * P * PACK], BF16, align_bytes=64, name="ht_grouped")
-            for j in range(PACK):
+            if k not in ht_grouped:
+                ht_grouped[k] = work.tile([P, PACK, FEATURE_PASSES * P * PACK], BF16, align_bytes=64, name="ht_grouped")
+            for j in frame_rows:
                 bank = psum_t.tile([P, 2, FEATURE_PASSES * P], F32, name="ht_bank")
                 for g in range(FEATURE_PASSES):
                     for u in range(2):
@@ -114,10 +115,9 @@ def tile_instrumentspecificslotmemory_pa_t_kernel(tc, H, Wr_words, Wr_scales, br
                             identity[:],
                         )
                 nc.scalar.copy(
-                    out=grouped[:].bitcast(F32)[:, j, :].rearrange("p (c u) -> p c u", u=2),
+                    out=ht_grouped[k][:].bitcast(F32)[:, j, :].rearrange("p (c u) -> p c u", u=2),
                     in_=bank[:].rearrange("p u c -> p c u"),
                 )
-            ht_grouped[k] = grouped
 
         def quantise_h(k):
             seq, part = divmod(k, CHUNKS_PER_SEQ)
@@ -140,9 +140,9 @@ def tile_instrumentspecificslotmemory_pa_t_kernel(tc, H, Wr_words, Wr_scales, br
             )
             ht_codes[k], ht_scales[k] = codes, scales
 
-        def route_chunk(k):
+        def route_logits(k):
             codes, scales = ht_codes[k], ht_scales[k]
-            logits = work.tile([P, SLOTS, PACK], F32, name="logits")
+            logits[k] = work.tile([P, SLOTS, PACK], F32, name="logits")
             for s in range(SLOT_TILES):
                 slots = slice(s * P, (s + 1) * P)
                 bank = psum_r.tile([P, PACK, P], F32, name="route_bank")
@@ -158,14 +158,15 @@ def tile_instrumentspecificslotmemory_pa_t_kernel(tc, H, Wr_words, Wr_scales, br
                             stop=(g == FEATURE_PASSES - 1),
                         )
                 nc.vector.tensor_tensor(
-                    out=logits[:, slots, :],
+                    out=logits[k][:, slots, :],
                     in0=bank[:].rearrange("p j n -> p n j"),
                     in1=bias[:, slots].unsqueeze(2).to_broadcast([P, P, PACK]),
                     op=ADD,
                 )
-            grouped = work.tile([P, SLOTS * PACK], BF16, align_bytes=64, name="route_grouped")
-            nc.scalar.activation(out=grouped[:], in_=logits[:].rearrange("p n j -> p (n j)"), func=SIGMOID)
-            route_grouped[k] = grouped
+
+        def sigmoid(k):
+            route_grouped[k] = work.tile([P, SLOTS * PACK], BF16, align_bytes=64, name="route_grouped")
+            nc.scalar.activation(out=route_grouped[k][:], in_=logits[k][:].rearrange("p n j -> p (n j)"), func=SIGMOID)
 
         def quantise_route(k):
             seq, part = divmod(k, CHUNKS_PER_SEQ)
@@ -210,19 +211,25 @@ def tile_instrumentspecificslotmemory_pa_t_kernel(tc, H, Wr_words, Wr_scales, br
         for k in range(N_CHUNKS + 4):
             if is_chunk(k + PREFETCH):
                 load(k + PREFETCH)
+            if is_chunk(k - 1):
+                quantise_ht(k - 1)
+            if is_chunk(k - 2):
+                quantise_h(k - 2)
+            if is_chunk(k - 1):
+                regroup_on_vector(k - 1)
+            if is_chunk(k):
+                transpose(k, range(0, PACK // 2))
+            if is_chunk(k - 2):
+                sigmoid(k - 2)
+            if is_chunk(k - 4):
+                aggregate(k - 4)
+            if is_chunk(k):
+                transpose(k, range(PACK // 2, PACK))
+            if is_chunk(k - 4):
+                drain_agg(k - 4)
+            if is_chunk(k - 1):
+                regroup_on_scalar(k - 1)
             if is_chunk(k - 2):
                 quantise_route(k - 2)
             if is_chunk(k - 1):
-                quantise_ht(k - 1)
-            if is_chunk(k):
-                regroup(k)
-            if is_chunk(k - 4):
-                drain_agg(k - 4)
-            if is_chunk(k):
-                transpose(k)
-            if is_chunk(k - 1):
-                route_chunk(k - 1)
-            if is_chunk(k):
-                quantise_h(k)
-            if is_chunk(k - 3):
-                aggregate(k - 3)
+                route_logits(k - 1)

@@ -10,6 +10,7 @@ U32 = mybir.dt.uint32
 U8 = mybir.dt.uint8
 FP8X4 = mybir.dt.float8_e4m3fn_x4
 ADD = mybir.AluOpType.add
+MULT = mybir.AluOpType.mult
 SIGMOID = mybir.ActivationFunctionType.Sigmoid
 
 SEQS, FRAMES, FEATURES, SLOTS = 8, 1024, 1024, 256
@@ -29,7 +30,8 @@ FEATURE_BANKS = FEATURES // BANK
 N_OUT_TILES = SEQS * SLOT_TILES
 assert N_OUT_TILES == N_CHUNKS
 
-VECTOR_FEATURES = FEATURES * 3 // 4
+VECTOR_END = FEATURES * 5 // 8
+GPSIMD_END = FEATURES * 7 // 8
 
 PREFETCH = 4
 
@@ -91,14 +93,24 @@ def tile_instrumentspecificslotmemory_pa_t_kernel(tc, H, Wr_words, Wr_scales, br
         def regroup_on_vector(k):
             h_grouped[k] = work.tile([P, FEATURES, PACK], BF16, align_bytes=64, name="h_grouped")
             nc.vector.tensor_copy(
-                out=h_grouped[k][:, :VECTOR_FEATURES, :].rearrange("p (c i) j -> p c j i", i=4),
-                in_=h_rows[k][:, :, :VECTOR_FEATURES].rearrange("p j (c i) -> p c j i", i=4),
+                out=h_grouped[k][:, :VECTOR_END, :].rearrange("p (c i) j -> p c j i", i=4),
+                in_=h_rows[k][:, :, :VECTOR_END].rearrange("p j (c i) -> p c j i", i=4),
+            )
+
+        def regroup_on_gpsimd(k):
+            nc.gpsimd.tensor_scalar(
+                out=h_grouped[k][:, VECTOR_END:GPSIMD_END, :],
+                in0=h_rows[k][:, :, VECTOR_END:GPSIMD_END].rearrange("p j d -> p d j"),
+                scalar1=1.0,
+                scalar2=0.0,
+                op0=MULT,
+                op1=ADD,
             )
 
         def regroup_on_scalar(k):
             nc.scalar.copy(
-                out=h_grouped[k][:, VECTOR_FEATURES:, :].rearrange("p (c i) j -> p c j i", i=4),
-                in_=h_rows[k][:, :, VECTOR_FEATURES:].rearrange("p j (c i) -> p c j i", i=4),
+                out=h_grouped[k][:, GPSIMD_END:, :].rearrange("p (c i) j -> p c j i", i=4),
+                in_=h_rows[k][:, :, GPSIMD_END:].rearrange("p j (c i) -> p c j i", i=4),
             )
 
         def transpose(k, frame_rows):
@@ -217,6 +229,7 @@ def tile_instrumentspecificslotmemory_pa_t_kernel(tc, H, Wr_words, Wr_scales, br
                 quantise_h(k - 2)
             if is_chunk(k - 1):
                 regroup_on_vector(k - 1)
+                regroup_on_gpsimd(k - 1)
             if is_chunk(k):
                 transpose(k, range(0, PACK // 2))
             if is_chunk(k - 2):

@@ -10,7 +10,6 @@ U32 = mybir.dt.uint32
 U8 = mybir.dt.uint8
 FP8X4 = mybir.dt.float8_e4m3fn_x4
 ADD = mybir.AluOpType.add
-MULT = mybir.AluOpType.mult
 SIGMOID = mybir.ActivationFunctionType.Sigmoid
 
 SEQS, FRAMES, FEATURES, SLOTS = 8, 1024, 1024, 256
@@ -30,8 +29,7 @@ FEATURE_BANKS = FEATURES // BANK
 N_OUT_TILES = SEQS * SLOT_TILES
 assert N_OUT_TILES == N_CHUNKS
 
-VECTOR_END = FEATURES * 5 // 8
-GPSIMD_END = FEATURES * 7 // 8
+VECTOR_FEATURES = FEATURES * 3 // 4
 
 PREFETCH = 4
 
@@ -49,7 +47,6 @@ def tile_instrumentspecificslotmemory_pa_t_kernel(tc, H, Wr_words, Wr_scales, br
         psum_t = stack.enter_context(tc.psum_pool(name="psum_t", bufs=4))
         psum_r = stack.enter_context(tc.psum_pool(name="psum_r", bufs=2))
         psum_a = stack.enter_context(tc.psum_pool(name="psum_a", bufs=2))
-        stack.enter_context(tc.manual_schedule())
 
         h_rows, h_grouped, ht_grouped, ht_codes, ht_scales, logits, route_grouped = {}, {}, {}, {}, {}, {}, {}
         h_codes, h_scales, route_codes, route_scales = {}, {}, {}, {}
@@ -93,24 +90,14 @@ def tile_instrumentspecificslotmemory_pa_t_kernel(tc, H, Wr_words, Wr_scales, br
         def regroup_on_vector(k):
             h_grouped[k] = work.tile([P, FEATURES, PACK], BF16, align_bytes=64, name="h_grouped")
             nc.vector.tensor_copy(
-                out=h_grouped[k][:, :VECTOR_END, :].rearrange("p (c i) j -> p c j i", i=4),
-                in_=h_rows[k][:, :, :VECTOR_END].rearrange("p j (c i) -> p c j i", i=4),
-            )
-
-        def regroup_on_gpsimd(k):
-            nc.gpsimd.tensor_scalar(
-                out=h_grouped[k][:, VECTOR_END:GPSIMD_END, :],
-                in0=h_rows[k][:, :, VECTOR_END:GPSIMD_END].rearrange("p j d -> p d j"),
-                scalar1=1.0,
-                scalar2=0.0,
-                op0=MULT,
-                op1=ADD,
+                out=h_grouped[k][:, :VECTOR_FEATURES, :].rearrange("p (c i) j -> p c j i", i=4),
+                in_=h_rows[k][:, :, :VECTOR_FEATURES].rearrange("p j (c i) -> p c j i", i=4),
             )
 
         def regroup_on_scalar(k):
             nc.scalar.copy(
-                out=h_grouped[k][:, GPSIMD_END:, :].rearrange("p (c i) j -> p c j i", i=4),
-                in_=h_rows[k][:, :, GPSIMD_END:].rearrange("p j (c i) -> p c j i", i=4),
+                out=h_grouped[k][:, VECTOR_FEATURES:, :].rearrange("p (c i) j -> p c j i", i=4),
+                in_=h_rows[k][:, :, VECTOR_FEATURES:].rearrange("p j (c i) -> p c j i", i=4),
             )
 
         def transpose(k, frame_rows):
@@ -229,7 +216,6 @@ def tile_instrumentspecificslotmemory_pa_t_kernel(tc, H, Wr_words, Wr_scales, br
                 quantise_h(k - 2)
             if is_chunk(k - 1):
                 regroup_on_vector(k - 1)
-                regroup_on_gpsimd(k - 1)
             if is_chunk(k):
                 transpose(k, range(0, PACK // 2))
             if is_chunk(k - 2):

@@ -33,6 +33,9 @@ VECTOR_FEATURES = FEATURES * 3 // 4
 
 PREFETCH = 4
 
+FIRST_ROWS = slice(0, PACK // 2)
+LAST_ROWS = slice(PACK // 2, PACK)
+
 FLOPS = 2 * 2 * SEQS * FRAMES * FEATURES * SLOTS
 
 
@@ -40,13 +43,13 @@ def tile_instrumentspecificslotmemory_pa_t_kernel(tc, H, Wr_words, Wr_scales, br
     nc = tc.nc
     with ExitStack() as stack:
         const = stack.enter_context(tc.tile_pool(name="const", bufs=1))
-        rows_pool = stack.enter_context(tc.tile_pool(name="rows", bufs=PREFETCH + 3))
+        rows_pool = stack.enter_context(tc.tile_pool(name="rows", bufs=PREFETCH + 2))
         work = stack.enter_context(tc.tile_pool(name="work", bufs=2))
         seq_pool = stack.enter_context(tc.tile_pool(name="seq", bufs=3))
-        out_pool = stack.enter_context(tc.tile_pool(name="out", bufs=3))
-        psum_t = stack.enter_context(tc.psum_pool(name="psum_t", bufs=4))
+        out_pool = stack.enter_context(tc.tile_pool(name="out", bufs=4))
         psum_r = stack.enter_context(tc.psum_pool(name="psum_r", bufs=2))
-        psum_a = stack.enter_context(tc.psum_pool(name="psum_a", bufs=2))
+        psum_ta = stack.enter_context(tc.psum_pool(name="psum_ta", bufs=6))
+        stack.enter_context(tc.manual_schedule())
 
         h_rows, h_grouped, ht_grouped, ht_codes, ht_scales, logits, route_grouped = {}, {}, {}, {}, {}, {}, {}
         h_codes, h_scales, route_codes, route_scales = {}, {}, {}, {}
@@ -55,8 +58,9 @@ def tile_instrumentspecificslotmemory_pa_t_kernel(tc, H, Wr_words, Wr_scales, br
         def load(k):
             seq, part = divmod(k, CHUNKS_PER_SEQ)
             rows = rows_pool.tile([P, PACK, FEATURES], BF16)
-            frames = H[seq, part * CHUNK : (part + 1) * CHUNK, :]
-            nc.sync.dma_start(out=rows[:], in_=frames.rearrange("(p j) d -> p j d", j=PACK))
+            frames = H[seq, part * CHUNK : (part + 1) * CHUNK, :].rearrange("(p j) d -> p j d", j=PACK)
+            for frame_rows in (FIRST_ROWS, LAST_ROWS):
+                nc.sync.dma_start(out=rows[:, frame_rows, :], in_=frames[:, frame_rows, :])
             h_rows[k] = rows
 
         load(0)
@@ -104,8 +108,8 @@ def tile_instrumentspecificslotmemory_pa_t_kernel(tc, H, Wr_words, Wr_scales, br
             words = h_rows[k][:].bitcast(F32)
             if k not in ht_grouped:
                 ht_grouped[k] = work.tile([P, PACK, FEATURE_PASSES * P * PACK], BF16, align_bytes=64, name="ht_grouped")
-            for j in frame_rows:
-                bank = psum_t.tile([P, 2, FEATURE_PASSES * P], F32, name="ht_bank")
+            for j in range(PACK)[frame_rows]:
+                bank = psum_ta.tile([P, 2, FEATURE_PASSES * P], F32, name="ht_bank", tag="bank")
                 for g in range(FEATURE_PASSES):
                     for u in range(2):
                         nc.tensor.transpose(
@@ -184,7 +188,7 @@ def tile_instrumentspecificslotmemory_pa_t_kernel(tc, H, Wr_words, Wr_scales, br
             agg_banks[t] = []
             for f in range(FEATURE_BANKS):
                 features = slice(f * BANK, (f + 1) * BANK)
-                bank = psum_a.tile([P, BANK], F32, name="agg_bank")
+                bank = psum_ta.tile([P, BANK], F32, name="agg_bank", tag="bank")
                 for part in range(CHUNKS_PER_SEQ):
                     nc.tensor.matmul_mx(
                         out=bank[:],
@@ -199,10 +203,10 @@ def tile_instrumentspecificslotmemory_pa_t_kernel(tc, H, Wr_words, Wr_scales, br
 
         def drain_agg(t):
             seq, s = divmod(t, SLOT_TILES)
-            result = out_pool.tile([P, FEATURES], F32)
             for f, bank in enumerate(agg_banks[t]):
-                nc.scalar.copy(out=result[:, f * BANK : (f + 1) * BANK], in_=bank[:])
-            nc.sync.dma_start(out=out[seq, s * P : (s + 1) * P, :], in_=result[:])
+                result = out_pool.tile([P, BANK], F32)
+                nc.scalar.copy(out=result[:], in_=bank[:])
+                nc.sync.dma_start(out=out[seq, s * P : (s + 1) * P, f * BANK : (f + 1) * BANK], in_=result[:])
 
         def is_chunk(i):
             return 0 <= i < N_CHUNKS
@@ -212,22 +216,20 @@ def tile_instrumentspecificslotmemory_pa_t_kernel(tc, H, Wr_words, Wr_scales, br
                 load(k + PREFETCH)
             if is_chunk(k - 1):
                 quantise_ht(k - 1)
-            if is_chunk(k - 2):
-                quantise_h(k - 2)
-            if is_chunk(k - 1):
-                regroup_on_vector(k - 1)
+                quantise_h(k - 1)
             if is_chunk(k):
-                transpose(k, range(0, PACK // 2))
+                regroup_on_vector(k)
+                transpose(k, FIRST_ROWS)
             if is_chunk(k - 2):
                 sigmoid(k - 2)
             if is_chunk(k - 4):
                 aggregate(k - 4)
             if is_chunk(k):
-                transpose(k, range(PACK // 2, PACK))
+                transpose(k, LAST_ROWS)
             if is_chunk(k - 4):
                 drain_agg(k - 4)
-            if is_chunk(k - 1):
-                regroup_on_scalar(k - 1)
+            if is_chunk(k):
+                regroup_on_scalar(k)
             if is_chunk(k - 2):
                 quantise_route(k - 2)
             if is_chunk(k - 1):

@@ -9,7 +9,6 @@ I32 = mybir.dt.int32
 U32 = mybir.dt.uint32
 U8 = mybir.dt.uint8
 FP8X4 = mybir.dt.float8_e4m3fn_x4
-ADD = mybir.AluOpType.add
 SIGMOID = mybir.ActivationFunctionType.Sigmoid
 
 SEQS, FRAMES, FEATURES, SLOTS = 8, 1024, 1024, 256
@@ -29,12 +28,7 @@ FEATURE_BANKS = FEATURES // BANK
 N_OUT_TILES = SEQS * SLOT_TILES
 assert N_OUT_TILES == N_CHUNKS
 
-VECTOR_FEATURES = FEATURES * 3 // 4
-
 PREFETCH = 4
-
-FIRST_ROWS = slice(0, PACK // 2)
-LAST_ROWS = slice(PACK // 2, PACK)
 
 FLOPS = 2 * 2 * SEQS * FRAMES * FEATURES * SLOTS
 
@@ -47,20 +41,19 @@ def tile_instrumentspecificslotmemory_pa_t_kernel(tc, H, Wr_words, Wr_scales, br
         work = stack.enter_context(tc.tile_pool(name="work", bufs=2))
         seq_pool = stack.enter_context(tc.tile_pool(name="seq", bufs=3))
         out_pool = stack.enter_context(tc.tile_pool(name="out", bufs=4))
-        psum_r = stack.enter_context(tc.psum_pool(name="psum_r", bufs=2))
-        psum_ta = stack.enter_context(tc.psum_pool(name="psum_ta", bufs=6))
+        psum = stack.enter_context(tc.psum_pool(name="psum", bufs=8))
         stack.enter_context(tc.manual_schedule())
 
-        h_rows, h_grouped, ht_grouped, ht_codes, ht_scales, logits, route_grouped = {}, {}, {}, {}, {}, {}, {}
+        h_rows, h_grouped, ht_grouped, ht_codes, ht_scales, route_t, route_grouped = {}, {}, {}, {}, {}, {}, {}
         h_codes, h_scales, route_codes, route_scales = {}, {}, {}, {}
-        agg_banks = {}
+        logit_banks, agg_banks = {}, {}
 
         def load(k):
             seq, part = divmod(k, CHUNKS_PER_SEQ)
             rows = rows_pool.tile([P, PACK, FEATURES], BF16)
             frames = H[seq, part * CHUNK : (part + 1) * CHUNK, :].rearrange("(p j) d -> p j d", j=PACK)
-            for frame_rows in (FIRST_ROWS, LAST_ROWS):
-                nc.sync.dma_start(out=rows[:, frame_rows, :], in_=frames[:, frame_rows, :])
+            for half in range(2):
+                nc.sync.dma_start(out=rows[:, 2 * half : 2 * half + 2, :], in_=frames[:, 2 * half : 2 * half + 2, :])
             h_rows[k] = rows
 
         load(0)
@@ -77,11 +70,12 @@ def tile_instrumentspecificslotmemory_pa_t_kernel(tc, H, Wr_words, Wr_scales, br
                 out=w_scales[32 * quadrant : 32 * quadrant + 4, :, :].bitcast(I32),
                 in_=Wr_scales[:, 4 * quadrant : 4 * quadrant + 4, :].rearrange("g r n -> r g n").bitcast(I32),
             )
+        bias = const.tile([P, SLOT_TILES, 16], BF16)
+        with nc.allow_non_contiguous_dma(reason="256 bias values, one to a partition"):
+            for s in range(SLOT_TILES):
+                nc.gpsimd.dma_start(out=bias[:, s, 0:1], in_=br[s * P : (s + 1) * P].unsqueeze(1))
         for k in range(1, PREFETCH):
             load(k)
-
-        bias = const.tile([P, SLOTS], BF16)
-        nc.scalar.dma_start(out=bias[:], in_=br.partition_broadcast(P))
 
         identity = const.tile([P, P], F32)
         make_identity(nc, identity[:])
@@ -91,35 +85,32 @@ def tile_instrumentspecificslotmemory_pa_t_kernel(tc, H, Wr_words, Wr_scales, br
         nc.vector.memset(warm_in[:], 0.0)
         nc.scalar.activation(out=warm_out[:], in_=warm_in[:], func=SIGMOID)
 
-        def regroup_on_vector(k):
+        def regroup(k):
             h_grouped[k] = work.tile([P, FEATURES, PACK], BF16, align_bytes=64, name="h_grouped")
             nc.vector.tensor_copy(
-                out=h_grouped[k][:, :VECTOR_FEATURES, :].rearrange("p (c i) j -> p c j i", i=4),
-                in_=h_rows[k][:, :, :VECTOR_FEATURES].rearrange("p j (c i) -> p c j i", i=4),
+                out=h_grouped[k][:].rearrange("p (c i) j -> p c j i", i=4),
+                in_=h_rows[k][:].rearrange("p j (c i) -> p c j i", i=4),
             )
 
-        def regroup_on_scalar(k):
-            nc.scalar.copy(
-                out=h_grouped[k][:, VECTOR_FEATURES:, :].rearrange("p (c i) j -> p c j i", i=4),
-                in_=h_rows[k][:, :, VECTOR_FEATURES:].rearrange("p j (c i) -> p c j i", i=4),
-            )
-
-        def transpose(k, frame_rows):
+        def transpose(k, half):
             words = h_rows[k][:].bitcast(F32)
             if k not in ht_grouped:
-                ht_grouped[k] = work.tile([P, PACK, FEATURE_PASSES * P * PACK], BF16, align_bytes=64, name="ht_grouped")
-            for j in range(PACK)[frame_rows]:
-                bank = psum_ta.tile([P, 2, FEATURE_PASSES * P], F32, name="ht_bank", tag="bank")
-                for g in range(FEATURE_PASSES):
+                ht_grouped[k] = work.tile(
+                    [P, FEATURE_PASSES, CHUNK, PACK], BF16, align_bytes=64, name="ht_grouped"
+                )
+            for g in range(FEATURE_PASSES):
+                bank = psum.tile([P, 2, 2, P], F32, name="ht_bank", tag="bank")
+                for jj in range(2):
                     for u in range(2):
                         nc.tensor.transpose(
-                            bank[:, u, g * P : (g + 1) * P],
-                            words[:, j, g * WORDS_PER_PASS + u : (g + 1) * WORDS_PER_PASS : 2],
+                            bank[:, u, jj, :],
+                            words[:, 2 * half + jj, g * WORDS_PER_PASS + u : (g + 1) * WORDS_PER_PASS : 2],
                             identity[:],
                         )
+                grouped_words = ht_grouped[k][:, g, :, :].rearrange("p c t -> p (c t)").bitcast(F32)
                 nc.scalar.copy(
-                    out=ht_grouped[k][:].bitcast(F32)[:, j, :].rearrange("p (c u) -> p c u", u=2),
-                    in_=bank[:].rearrange("p u c -> p c u"),
+                    out=grouped_words[:, half * BANK : (half + 1) * BANK].rearrange("p (c u) -> p c u", u=2),
+                    in_=bank[:].rearrange("p u j c -> p (j c) u"),
                 )
 
         def quantise_h(k):
@@ -134,42 +125,56 @@ def tile_instrumentspecificslotmemory_pa_t_kernel(tc, H, Wr_words, Wr_scales, br
             )
 
         def quantise_ht(k):
-            codes = work.tile([P, PACK, FEATURE_PASSES, P], U32, align_bytes=64, name="ht_codes")
-            scales = work.tile([P, PACK, FEATURE_PASSES, P], U8, align_bytes=64, name="ht_scales")
+            codes = work.tile([P, FEATURE_PASSES, CHUNK], U32, align_bytes=64, name="ht_codes")
+            scales = work.tile([P, FEATURE_PASSES, CHUNK], U8, align_bytes=64, name="ht_scales")
             nc.vector.quantize_mx(
-                out=codes[:].rearrange("p j g c -> p (j g c)").bitcast(FP8X4),
-                scales=scales[:].rearrange("p j g c -> p (j g c)"),
-                in_=ht_grouped[k][:].rearrange("p j c -> p (j c)"),
+                out=codes[:].rearrange("p g c -> p (g c)").bitcast(FP8X4),
+                scales=scales[:].rearrange("p g c -> p (g c)"),
+                in_=ht_grouped[k][:].rearrange("p g c t -> p (g c t)"),
             )
             ht_codes[k], ht_scales[k] = codes, scales
 
         def route_logits(k):
             codes, scales = ht_codes[k], ht_scales[k]
-            logits[k] = work.tile([P, SLOTS, PACK], F32, name="logits")
+            logit_banks[k] = []
             for s in range(SLOT_TILES):
                 slots = slice(s * P, (s + 1) * P)
-                bank = psum_r.tile([P, PACK, P], F32, name="route_bank")
-                for j in range(PACK):
-                    for g in range(FEATURE_PASSES):
-                        nc.tensor.matmul_mx(
-                            out=bank[:, j, :],
-                            lhsT=codes[:, j, g, :].bitcast(FP8X4),
-                            lhsT_scale=scales[:, j, g, :],
-                            rhs=w_words[:, g, slots].bitcast(FP8X4),
-                            rhs_scale=w_scales[:, g, slots],
-                            start=(g == 0),
-                            stop=(g == FEATURE_PASSES - 1),
-                        )
-                nc.vector.tensor_tensor(
-                    out=logits[k][:, slots, :],
-                    in0=bank[:].rearrange("p j n -> p n j"),
-                    in1=bias[:, slots].unsqueeze(2).to_broadcast([P, P, PACK]),
-                    op=ADD,
-                )
+                bank = psum.tile([P, CHUNK], F32, name="logit_bank", tag="bank")
+                for g in range(FEATURE_PASSES):
+                    nc.tensor.matmul_mx(
+                        out=bank[:],
+                        lhsT=w_words[:, g, slots].bitcast(FP8X4),
+                        lhsT_scale=w_scales[:, g, slots],
+                        rhs=codes[:, g, :].bitcast(FP8X4),
+                        rhs_scale=scales[:, g, :],
+                        start=(g == 0),
+                        stop=(g == FEATURE_PASSES - 1),
+                    )
+                logit_banks[k].append(bank)
 
         def sigmoid(k):
-            route_grouped[k] = work.tile([P, SLOTS * PACK], BF16, align_bytes=64, name="route_grouped")
-            nc.scalar.activation(out=route_grouped[k][:], in_=logits[k][:].rearrange("p n j -> p (n j)"), func=SIGMOID)
+            route_t[k] = work.tile([P, SLOT_TILES, CHUNK], BF16, align_bytes=64, name="route_t")
+            for s, bank in enumerate(logit_banks[k]):
+                nc.scalar.activation(
+                    out=route_t[k][:, s, :].rearrange("p (u c e) -> p u c e", u=2, e=2),
+                    in_=bank[:].rearrange("p (u e c) -> p u c e", u=2, e=2),
+                    func=SIGMOID,
+                    bias=bias[:, s, 0:1],
+                )
+
+        def transpose_route(k):
+            words = route_t[k][:].bitcast(F32)
+            bank = psum.tile([P, 2, SLOTS], F32, name="route_bank", tag="bank")
+            for s in range(SLOT_TILES):
+                for u in range(2):
+                    nc.tensor.transpose(
+                        bank[:, u, s * P : (s + 1) * P], words[:, s, u * P : (u + 1) * P], identity[:]
+                    )
+            route_grouped[k] = work.tile([P, SLOTS, PACK], BF16, align_bytes=64, name="route_grouped")
+            nc.scalar.copy(
+                out=route_grouped[k][:].rearrange("p n j -> p (n j)").bitcast(F32).rearrange("p (n u) -> p n u", u=2),
+                in_=bank[:].rearrange("p u n -> p n u"),
+            )
 
         def quantise_route(k):
             seq, part = divmod(k, CHUNKS_PER_SEQ)
@@ -179,7 +184,7 @@ def tile_instrumentspecificslotmemory_pa_t_kernel(tc, H, Wr_words, Wr_scales, br
             nc.vector.quantize_mx(
                 out=route_codes[seq][:, part, :].bitcast(FP8X4),
                 scales=route_scales[seq][:, part, :],
-                in_=route_grouped[k][:],
+                in_=route_grouped[k][:].rearrange("p n j -> p (n j)"),
             )
 
         def aggregate(t):
@@ -188,7 +193,7 @@ def tile_instrumentspecificslotmemory_pa_t_kernel(tc, H, Wr_words, Wr_scales, br
             agg_banks[t] = []
             for f in range(FEATURE_BANKS):
                 features = slice(f * BANK, (f + 1) * BANK)
-                bank = psum_ta.tile([P, BANK], F32, name="agg_bank", tag="bank")
+                bank = psum.tile([P, BANK], F32, name="agg_bank", tag="bank")
                 for part in range(CHUNKS_PER_SEQ):
                     nc.tensor.matmul_mx(
                         out=bank[:],
@@ -216,21 +221,20 @@ def tile_instrumentspecificslotmemory_pa_t_kernel(tc, H, Wr_words, Wr_scales, br
                 load(k + PREFETCH)
             if is_chunk(k - 1):
                 quantise_ht(k - 1)
+            if is_chunk(k - 3):
+                quantise_route(k - 3)
+            if is_chunk(k - 1):
                 quantise_h(k - 1)
             if is_chunk(k):
-                regroup_on_vector(k)
-                transpose(k, FIRST_ROWS)
-            if is_chunk(k - 2):
-                sigmoid(k - 2)
+                regroup(k)
+                transpose(k, 0)
             if is_chunk(k - 4):
                 aggregate(k - 4)
-            if is_chunk(k):
-                transpose(k, LAST_ROWS)
-            if is_chunk(k - 4):
                 drain_agg(k - 4)
             if is_chunk(k):
-                regroup_on_scalar(k)
+                transpose(k, 1)
             if is_chunk(k - 2):
-                quantise_route(k - 2)
+                transpose_route(k - 2)
             if is_chunk(k - 1):
                 route_logits(k - 1)
+                sigmoid(k - 1)

@@ -1,4 +1,5 @@
 from contextlib import ExitStack
+from itertools import product
 
 import concourse.mybir as mybir
 from concourse.masks import make_identity
@@ -28,6 +29,8 @@ FEATURE_BANKS = FEATURES // BANK
 N_OUT_TILES = SEQS * SLOT_TILES
 assert N_OUT_TILES == N_CHUNKS
 
+FEATURE_HALVES = (slice(0, FEATURES // 2), slice(FEATURES // 2, FEATURES))
+
 PREFETCH = 4
 
 FLOPS = 2 * 2 * SEQS * FRAMES * FEATURES * SLOTS
@@ -37,9 +40,10 @@ def tile_instrumentspecificslotmemory_pa_t_kernel(tc, H, Wr_words, Wr_scales, br
     nc = tc.nc
     with ExitStack() as stack:
         const = stack.enter_context(tc.tile_pool(name="const", bufs=1))
-        rows_pool = stack.enter_context(tc.tile_pool(name="rows", bufs=PREFETCH + 2))
+        rows_pool = stack.enter_context(tc.tile_pool(name="rows", bufs=PREFETCH + 4))
         work = stack.enter_context(tc.tile_pool(name="work", bufs=2))
         seq_pool = stack.enter_context(tc.tile_pool(name="seq", bufs=3))
+        grouped_pool = stack.enter_context(tc.tile_pool(name="grouped", bufs=3))
         out_pool = stack.enter_context(tc.tile_pool(name="out", bufs=4))
         psum = stack.enter_context(tc.psum_pool(name="psum", bufs=8))
         stack.enter_context(tc.manual_schedule())
@@ -52,11 +56,12 @@ def tile_instrumentspecificslotmemory_pa_t_kernel(tc, H, Wr_words, Wr_scales, br
             seq, part = divmod(k, CHUNKS_PER_SEQ)
             rows = rows_pool.tile([P, PACK, FEATURES], BF16)
             frames = H[seq, part * CHUNK : (part + 1) * CHUNK, :].rearrange("(p j) d -> p j d", j=PACK)
-            for half in range(2):
-                nc.sync.dma_start(out=rows[:, 2 * half : 2 * half + 2, :], in_=frames[:, 2 * half : 2 * half + 2, :])
+            for features in FEATURE_HALVES if k == 0 else (slice(0, FEATURES),):
+                nc.sync.dma_start(out=rows[:, :, features], in_=frames[:, :, features])
             h_rows[k] = rows
 
         load(0)
+        load(1)
 
         w_words = const.tile([P, FEATURE_PASSES, SLOTS], U32, align_bytes=64)
         nc.sync.dma_start(
@@ -74,7 +79,7 @@ def tile_instrumentspecificslotmemory_pa_t_kernel(tc, H, Wr_words, Wr_scales, br
         with nc.allow_non_contiguous_dma(reason="256 bias values, one to a partition"):
             for s in range(SLOT_TILES):
                 nc.gpsimd.dma_start(out=bias[:, s, 0:1], in_=br[s * P : (s + 1) * P].unsqueeze(1))
-        for k in range(1, PREFETCH):
+        for k in range(2, PREFETCH):
             load(k)
 
         identity = const.tile([P, P], F32)
@@ -85,20 +90,19 @@ def tile_instrumentspecificslotmemory_pa_t_kernel(tc, H, Wr_words, Wr_scales, br
         nc.vector.memset(warm_in[:], 0.0)
         nc.scalar.activation(out=warm_out[:], in_=warm_in[:], func=SIGMOID)
 
-        def regroup(k):
-            h_grouped[k] = work.tile([P, FEATURES, PACK], BF16, align_bytes=64, name="h_grouped")
+        def regroup(k, half):
+            if half == 0:
+                h_grouped[k] = grouped_pool.tile([P, FEATURES, PACK], BF16, align_bytes=64, name="h_grouped")
+            features = FEATURE_HALVES[half]
             nc.vector.tensor_copy(
-                out=h_grouped[k][:].rearrange("p (c i) j -> p c j i", i=4),
-                in_=h_rows[k][:].rearrange("p j (c i) -> p c j i", i=4),
+                out=h_grouped[k][:, features, :].rearrange("p (c i) j -> p c j i", i=4),
+                in_=h_rows[k][:, :, features].rearrange("p j (c i) -> p c j i", i=4),
             )
 
-        def transpose(k, half):
+        def transpose(k):
             words = h_rows[k][:].bitcast(F32)
-            if k not in ht_grouped:
-                ht_grouped[k] = work.tile(
-                    [P, FEATURE_PASSES, CHUNK, PACK], BF16, align_bytes=64, name="ht_grouped"
-                )
-            for g in range(FEATURE_PASSES):
+            ht_grouped[k] = work.tile([P, FEATURE_PASSES, CHUNK, PACK], BF16, align_bytes=64, name="ht_grouped")
+            for g, half in product(range(FEATURE_PASSES), range(2)):
                 bank = psum.tile([P, 2, 2, P], F32, name="ht_bank", tag="bank")
                 for jj in range(2):
                     for u in range(2):
@@ -216,6 +220,10 @@ def tile_instrumentspecificslotmemory_pa_t_kernel(tc, H, Wr_words, Wr_scales, br
         def is_chunk(i):
             return 0 <= i < N_CHUNKS
 
+        pieces = []
+        for k in range(N_CHUNKS):
+            pieces += [(regroup, k, 0), (regroup, k, 1), (quantise_h, k)]
+
         for k in range(N_CHUNKS + 4):
             if is_chunk(k + PREFETCH):
                 load(k + PREFETCH)
@@ -223,18 +231,16 @@ def tile_instrumentspecificslotmemory_pa_t_kernel(tc, H, Wr_words, Wr_scales, br
                 quantise_ht(k - 1)
             if is_chunk(k - 3):
                 quantise_route(k - 3)
-            if is_chunk(k - 1):
-                quantise_h(k - 1)
+            for piece, *where in pieces[: 2 if k < 4 else 3]:
+                piece(*where)
+            pieces = pieces[2 if k < 4 else 3 :]
             if is_chunk(k):
-                regroup(k)
-                transpose(k, 0)
-            if is_chunk(k - 4):
-                aggregate(k - 4)
-                drain_agg(k - 4)
-            if is_chunk(k):
-                transpose(k, 1)
+                transpose(k)
             if is_chunk(k - 2):
                 transpose_route(k - 2)
             if is_chunk(k - 1):
                 route_logits(k - 1)
                 sigmoid(k - 1)
+            if is_chunk(k - 4):
+                aggregate(k - 4)
+                drain_agg(k - 4)

@@ -41,6 +41,7 @@ def tile_instrumentspecificslotmemory_pa_t_kernel(tc, H, Wr_words, Wr_scales, br
     with ExitStack() as stack:
         const = stack.enter_context(tc.tile_pool(name="const", bufs=1))
         rows_pool = stack.enter_context(tc.tile_pool(name="rows", bufs=PREFETCH + 4))
+        first_pool = stack.enter_context(tc.tile_pool(name="first", bufs=2))
         work = stack.enter_context(tc.tile_pool(name="work", bufs=2))
         seq_pool = stack.enter_context(tc.tile_pool(name="seq", bufs=3))
         grouped_pool = stack.enter_context(tc.tile_pool(name="grouped", bufs=3))
@@ -50,15 +51,22 @@ def tile_instrumentspecificslotmemory_pa_t_kernel(tc, H, Wr_words, Wr_scales, br
 
         h_rows, h_grouped, ht_grouped, ht_codes, ht_scales, route_t, route_grouped = {}, {}, {}, {}, {}, {}, {}
         h_codes, h_scales, route_codes, route_scales = {}, {}, {}, {}
-        logit_banks, agg_banks = {}, {}
+        logit_banks = {}
 
         def load(k):
             seq, part = divmod(k, CHUNKS_PER_SEQ)
-            rows = rows_pool.tile([P, PACK, FEATURES], BF16)
             frames = H[seq, part * CHUNK : (part + 1) * CHUNK, :].rearrange("(p j) d -> p j d", j=PACK)
-            for features in FEATURE_HALVES if k == 0 else (slice(0, FEATURES),):
-                nc.sync.dma_start(out=rows[:, :, features], in_=frames[:, :, features])
-            h_rows[k] = rows
+            if k < 2:
+                rows = first_pool.tile([P, 2, PACK, FEATURES // 2], BF16)
+                for half, j in product(range(2), (0, PACK // 2)):
+                    nc.sync.dma_start(
+                        out=rows[:, half, j : j + 2, :], in_=frames[:, j : j + 2, FEATURE_HALVES[half]]
+                    )
+                h_rows[k] = [rows[:, half, :, :] for half in range(2)]
+            else:
+                rows = rows_pool.tile([P, PACK, FEATURES], BF16)
+                nc.sync.dma_start(out=rows[:], in_=frames)
+                h_rows[k] = [rows[:, :, features] for features in FEATURE_HALVES]
 
         load(0)
         load(1)
@@ -75,32 +83,30 @@ def tile_instrumentspecificslotmemory_pa_t_kernel(tc, H, Wr_words, Wr_scales, br
                 out=w_scales[32 * quadrant : 32 * quadrant + 4, :, :].bitcast(I32),
                 in_=Wr_scales[:, 4 * quadrant : 4 * quadrant + 4, :].rearrange("g r n -> r g n").bitcast(I32),
             )
+        identity = const.tile([P, P], F32)
+        make_identity(nc, identity[:])
+
         bias = const.tile([P, SLOT_TILES, 16], BF16)
         with nc.allow_non_contiguous_dma(reason="256 bias values, one to a partition"):
             for s in range(SLOT_TILES):
-                nc.gpsimd.dma_start(out=bias[:, s, 0:1], in_=br[s * P : (s + 1) * P].unsqueeze(1))
+                nc.scalar.dma_start(out=bias[:, s, 0:1], in_=br[s * P : (s + 1) * P].unsqueeze(1))
         for k in range(2, PREFETCH):
             load(k)
-
-        identity = const.tile([P, P], F32)
-        make_identity(nc, identity[:])
 
         warm_in = const.tile([P, 1], F32)
         warm_out = const.tile([P, 1], F32)
         nc.vector.memset(warm_in[:], 0.0)
         nc.scalar.activation(out=warm_out[:], in_=warm_in[:], func=SIGMOID)
 
-        def regroup(k, half):
-            if half == 0:
-                h_grouped[k] = grouped_pool.tile([P, FEATURES, PACK], BF16, align_bytes=64, name="h_grouped")
-            features = FEATURE_HALVES[half]
-            nc.vector.tensor_copy(
-                out=h_grouped[k][:, features, :].rearrange("p (c i) j -> p c j i", i=4),
-                in_=h_rows[k][:, :, features].rearrange("p j (c i) -> p c j i", i=4),
+        def regroup(copy, k, half, start=0, stop=FEATURES // 2):
+            if k not in h_grouped:
+                h_grouped[k] = grouped_pool.tile([P, 2, FEATURES // 2, PACK], BF16, align_bytes=64, name="h_grouped")
+            copy(
+                out=h_grouped[k][:, half, start:stop, :].rearrange("p (c i) j -> p c j i", i=4),
+                in_=h_rows[k][half][:, :, start:stop].rearrange("p j (c i) -> p c j i", i=4),
             )
 
         def transpose(k):
-            words = h_rows[k][:].bitcast(F32)
             ht_grouped[k] = work.tile([P, FEATURE_PASSES, CHUNK, PACK], BF16, align_bytes=64, name="ht_grouped")
             for g, half in product(range(FEATURE_PASSES), range(2)):
                 bank = psum.tile([P, 2, 2, P], F32, name="ht_bank", tag="bank")
@@ -108,7 +114,7 @@ def tile_instrumentspecificslotmemory_pa_t_kernel(tc, H, Wr_words, Wr_scales, br
                     for u in range(2):
                         nc.tensor.transpose(
                             bank[:, u, jj, :],
-                            words[:, 2 * half + jj, g * WORDS_PER_PASS + u : (g + 1) * WORDS_PER_PASS : 2],
+                            h_rows[k][g].bitcast(F32)[:, 2 * half + jj, u:WORDS_PER_PASS:2],
                             identity[:],
                         )
                 grouped_words = ht_grouped[k][:, g, :, :].rearrange("p c t -> p (c t)").bitcast(F32)
@@ -117,15 +123,15 @@ def tile_instrumentspecificslotmemory_pa_t_kernel(tc, H, Wr_words, Wr_scales, br
                     in_=bank[:].rearrange("p u j c -> p (j c) u"),
                 )
 
-        def quantise_h(k):
+        def quantise_h(k, features):
             seq, part = divmod(k, CHUNKS_PER_SEQ)
-            if part == 0:
+            if part == 0 and features.start == 0:
                 h_codes[seq] = seq_pool.tile([P, CHUNKS_PER_SEQ, FEATURES], U32, align_bytes=64, name="h_codes")
                 h_scales[seq] = seq_pool.tile([P, CHUNKS_PER_SEQ, FEATURES], U8, align_bytes=64, name="h_scales")
             nc.vector.quantize_mx(
-                out=h_codes[seq][:, part, :].bitcast(FP8X4),
-                scales=h_scales[seq][:, part, :],
-                in_=h_grouped[k][:].rearrange("p d j -> p (d j)"),
+                out=h_codes[seq][:, part, features].bitcast(FP8X4),
+                scales=h_scales[seq][:, part, features],
+                in_=h_grouped[k][:].rearrange("p h d j -> p (h d) j")[:, features, :].rearrange("p d j -> p (d j)"),
             )
 
         def quantise_ht(k):
@@ -191,38 +197,40 @@ def tile_instrumentspecificslotmemory_pa_t_kernel(tc, H, Wr_words, Wr_scales, br
                 in_=route_grouped[k][:].rearrange("p n j -> p (n j)"),
             )
 
-        def aggregate(t):
+        def aggregate(t, f):
             seq, s = divmod(t, SLOT_TILES)
             slots = slice(s * P, (s + 1) * P)
-            agg_banks[t] = []
-            for f in range(FEATURE_BANKS):
-                features = slice(f * BANK, (f + 1) * BANK)
-                bank = psum.tile([P, BANK], F32, name="agg_bank", tag="bank")
-                for part in range(CHUNKS_PER_SEQ):
-                    nc.tensor.matmul_mx(
-                        out=bank[:],
-                        lhsT=route_codes[seq][:, part, slots].bitcast(FP8X4),
-                        lhsT_scale=route_scales[seq][:, part, slots],
-                        rhs=h_codes[seq][:, part, features].bitcast(FP8X4),
-                        rhs_scale=h_scales[seq][:, part, features],
-                        start=(part == 0),
-                        stop=(part == CHUNKS_PER_SEQ - 1),
-                    )
-                agg_banks[t].append(bank)
-
-        def drain_agg(t):
-            seq, s = divmod(t, SLOT_TILES)
-            for f, bank in enumerate(agg_banks[t]):
-                result = out_pool.tile([P, BANK], F32)
-                nc.scalar.copy(out=result[:], in_=bank[:])
-                nc.sync.dma_start(out=out[seq, s * P : (s + 1) * P, f * BANK : (f + 1) * BANK], in_=result[:])
+            features = FEATURE_HALVES[f]
+            bank = psum.tile([P, BANK], F32, name="agg_bank", tag="bank")
+            for part in range(CHUNKS_PER_SEQ):
+                nc.tensor.matmul_mx(
+                    out=bank[:],
+                    lhsT=route_codes[seq][:, part, slots].bitcast(FP8X4),
+                    lhsT_scale=route_scales[seq][:, part, slots],
+                    rhs=h_codes[seq][:, part, features].bitcast(FP8X4),
+                    rhs_scale=h_scales[seq][:, part, features],
+                    start=(part == 0),
+                    stop=(part == CHUNKS_PER_SEQ - 1),
+                )
+            result = out_pool.tile([P, BANK], F32)
+            nc.scalar.copy(out=result[:], in_=bank[:])
+            nc.sync.dma_start(out=out[seq, s * P : (s + 1) * P, features], in_=result[:])
 
         def is_chunk(i):
             return 0 <= i < N_CHUNKS
 
         pieces = []
-        for k in range(N_CHUNKS):
-            pieces += [(regroup, k, 0), (regroup, k, 1), (quantise_h, k)]
+        for k in range(N_CHUNKS - 1):
+            pieces += [(regroup, nc.vector.tensor_copy, k, half) for half in range(2)]
+            pieces.append((quantise_h, k, slice(0, FEATURES)))
+        last = N_CHUNKS - 1
+        pieces += [
+            (regroup, nc.vector.tensor_copy, last, 0),
+            (quantise_h, last, FEATURE_HALVES[0]),
+            (regroup, nc.vector.tensor_copy, last, 1, 0, FEATURES // 4),
+            (quantise_h, last, FEATURE_HALVES[1]),
+        ]
+        pieces_in_step = [3, 1, 2, 2] + [3] * (N_CHUNKS - 5) + [1, 2, 2, len(pieces)]
 
         for k in range(N_CHUNKS + 4):
             if is_chunk(k + PREFETCH):
@@ -231,16 +239,23 @@ def tile_instrumentspecificslotmemory_pa_t_kernel(tc, H, Wr_words, Wr_scales, br
                 quantise_ht(k - 1)
             if is_chunk(k - 3):
                 quantise_route(k - 3)
-            for piece, *where in pieces[: 2 if k < 4 else 3]:
-                piece(*where)
-            pieces = pieces[2 if k < 4 else 3 :]
+            if k < len(pieces_in_step):
+                for piece, *where in pieces[: pieces_in_step[k]]:
+                    piece(*where)
+                pieces = pieces[pieces_in_step[k] :]
             if is_chunk(k):
                 transpose(k)
             if is_chunk(k - 2):
                 transpose_route(k - 2)
+            if k - 1 == last:
+                regroup(nc.scalar.copy, last, 1, FEATURES // 4, FEATURES // 2)
             if is_chunk(k - 1):
                 route_logits(k - 1)
                 sigmoid(k - 1)
-            if is_chunk(k - 4):
-                aggregate(k - 4)
-                drain_agg(k - 4)
+            if is_chunk(k - 4) and k - 4 < N_OUT_TILES - 2:
+                for f in range(FEATURE_BANKS):
+                    aggregate(k - 4, f)
+            if k - 4 == N_OUT_TILES - 1:
+                for f in range(FEATURE_BANKS):
+                    aggregate(k - 5, f)
+                    aggregate(k - 4, f)

@@ -42,10 +42,10 @@ def tile_instrumentspecificslotmemory_pa_t_kernel(tc, H, Wr_words, Wr_scales, br
         const = stack.enter_context(tc.tile_pool(name="const", bufs=1))
         rows_pool = stack.enter_context(tc.tile_pool(name="rows", bufs=PREFETCH + 4))
         first_pool = stack.enter_context(tc.tile_pool(name="first", bufs=2))
-        work = stack.enter_context(tc.tile_pool(name="work", bufs=2))
+        work = stack.enter_context(tc.tile_pool(name="work", bufs=3))
         seq_pool = stack.enter_context(tc.tile_pool(name="seq", bufs=3))
         grouped_pool = stack.enter_context(tc.tile_pool(name="grouped", bufs=3))
-        out_pool = stack.enter_context(tc.tile_pool(name="out", bufs=4))
+        out_pool = stack.enter_context(tc.tile_pool(name="out", bufs=8))
         psum = stack.enter_context(tc.psum_pool(name="psum", bufs=8))
         stack.enter_context(tc.manual_schedule())
 
@@ -197,11 +197,11 @@ def tile_instrumentspecificslotmemory_pa_t_kernel(tc, H, Wr_words, Wr_scales, br
                 in_=route_grouped[k][:].rearrange("p n j -> p (n j)"),
             )
 
-        def aggregate(t, f):
+        def aggregate(t, features, copy):
             seq, s = divmod(t, SLOT_TILES)
             slots = slice(s * P, (s + 1) * P)
-            features = FEATURE_HALVES[f]
-            bank = psum.tile([P, BANK], F32, name="agg_bank", tag="bank")
+            width = features.stop - features.start
+            bank = psum.tile([P, width], F32, name="agg_bank", tag="bank")
             for part in range(CHUNKS_PER_SEQ):
                 nc.tensor.matmul_mx(
                     out=bank[:],
@@ -212,23 +212,29 @@ def tile_instrumentspecificslotmemory_pa_t_kernel(tc, H, Wr_words, Wr_scales, br
                     start=(part == 0),
                     stop=(part == CHUNKS_PER_SEQ - 1),
                 )
-            result = out_pool.tile([P, BANK], F32)
-            nc.scalar.copy(out=result[:], in_=bank[:])
+            result = out_pool.tile([P, width], F32)
+            copy(out=result[:], in_=bank[:])
             nc.sync.dma_start(out=out[seq, s * P : (s + 1) * P, features], in_=result[:])
 
         def is_chunk(i):
             return 0 <= i < N_CHUNKS
 
+        last = N_CHUNKS - 1
+        quarter = FEATURES // 4
+        scalar_quarters = (1, last)
+
         pieces = []
         for k in range(N_CHUNKS - 1):
-            pieces += [(regroup, nc.vector.tensor_copy, k, half) for half in range(2)]
+            pieces.append((regroup, nc.vector.tensor_copy, k, 0))
+            pieces.append((regroup, nc.vector.tensor_copy, k, 1, 0, quarter if k in scalar_quarters else 2 * quarter))
             pieces.append((quantise_h, k, slice(0, FEATURES)))
-        last = N_CHUNKS - 1
+        last_features = [FEATURE_HALVES[0], slice(3 * quarter, FEATURES), slice(2 * quarter, 3 * quarter)]
         pieces += [
             (regroup, nc.vector.tensor_copy, last, 0),
-            (quantise_h, last, FEATURE_HALVES[0]),
-            (regroup, nc.vector.tensor_copy, last, 1, 0, FEATURES // 4),
-            (quantise_h, last, FEATURE_HALVES[1]),
+            (quantise_h, last, last_features[0]),
+            (regroup, nc.vector.tensor_copy, last, 1, 0, quarter),
+            (quantise_h, last, last_features[1]),
+            (quantise_h, last, last_features[2]),
         ]
         pieces_in_step = [3, 1, 2, 2] + [3] * (N_CHUNKS - 5) + [1, 2, 2, len(pieces)]
 
@@ -247,15 +253,15 @@ def tile_instrumentspecificslotmemory_pa_t_kernel(tc, H, Wr_words, Wr_scales, br
                 transpose(k)
             if is_chunk(k - 2):
                 transpose_route(k - 2)
-            if k - 1 == last:
-                regroup(nc.scalar.copy, last, 1, FEATURES // 4, FEATURES // 2)
+            if k == 1 or k == last + 1:
+                regroup(nc.scalar.copy, min(k, last), 1, quarter, 2 * quarter)
             if is_chunk(k - 1):
                 route_logits(k - 1)
                 sigmoid(k - 1)
             if is_chunk(k - 4) and k - 4 < N_OUT_TILES - 2:
-                for f in range(FEATURE_BANKS):
-                    aggregate(k - 4, f)
+                for features in FEATURE_HALVES:
+                    aggregate(k - 4, features, nc.scalar.copy)
             if k - 4 == N_OUT_TILES - 1:
-                for f in range(FEATURE_BANKS):
-                    aggregate(k - 5, f)
-                    aggregate(k - 4, f)
+                for i, features in enumerate(last_features):
+                    aggregate(k - 5, features, nc.scalar.copy if i == 0 else nc.vector.tensor_copy)
+                    aggregate(k - 4, features, nc.scalar.copy)

@@ -33,6 +33,8 @@ FEATURE_HALVES = (slice(0, FEATURES // 2), slice(FEATURES // 2, FEATURES))
 
 PREFETCH = 4
 
+AGG_LAG = 5
+
 FLOPS = 2 * 2 * SEQS * FRAMES * FEATURES * SLOTS
 
 
@@ -62,11 +64,16 @@ def tile_instrumentspecificslotmemory_pa_t_kernel(tc, H, Wr_words, Wr_scales, br
                     nc.sync.dma_start(
                         out=rows[:, half, j : j + 2, :], in_=frames[:, j : j + 2, FEATURE_HALVES[half]]
                     )
-                h_rows[k] = [rows[:, half, :, :] for half in range(2)]
             else:
                 rows = rows_pool.tile([P, PACK, FEATURES], BF16)
                 nc.sync.dma_start(out=rows[:], in_=frames)
-                h_rows[k] = [rows[:, :, features] for features in FEATURE_HALVES]
+            h_rows[k] = rows
+
+        def rows_of(k, features):
+            if k < 2:
+                half, start = divmod(features.start, FEATURES // 2)
+                return h_rows[k][:, half, :, start : start + features.stop - features.start]
+            return h_rows[k][:, :, features]
 
         load(0)
         load(1)
@@ -98,12 +105,12 @@ def tile_instrumentspecificslotmemory_pa_t_kernel(tc, H, Wr_words, Wr_scales, br
         nc.vector.memset(warm_in[:], 0.0)
         nc.scalar.activation(out=warm_out[:], in_=warm_in[:], func=SIGMOID)
 
-        def regroup(copy, k, half, start=0, stop=FEATURES // 2):
+        def regroup(copy, k, features):
             if k not in h_grouped:
-                h_grouped[k] = grouped_pool.tile([P, 2, FEATURES // 2, PACK], BF16, align_bytes=64, name="h_grouped")
+                h_grouped[k] = grouped_pool.tile([P, FEATURES, PACK], BF16, align_bytes=64, name="h_grouped")
             copy(
-                out=h_grouped[k][:, half, start:stop, :].rearrange("p (c i) j -> p c j i", i=4),
-                in_=h_rows[k][half][:, :, start:stop].rearrange("p j (c i) -> p c j i", i=4),
+                out=h_grouped[k][:, features, :].rearrange("p (c i) j -> p c j i", i=4),
+                in_=rows_of(k, features).rearrange("p j (c i) -> p c j i", i=4),
             )
 
         def transpose(k):
@@ -114,7 +121,7 @@ def tile_instrumentspecificslotmemory_pa_t_kernel(tc, H, Wr_words, Wr_scales, br
                     for u in range(2):
                         nc.tensor.transpose(
                             bank[:, u, jj, :],
-                            h_rows[k][g].bitcast(F32)[:, 2 * half + jj, u:WORDS_PER_PASS:2],
+                            rows_of(k, FEATURE_HALVES[g]).bitcast(F32)[:, 2 * half + jj, u:WORDS_PER_PASS:2],
                             identity[:],
                         )
                 grouped_words = ht_grouped[k][:, g, :, :].rearrange("p c t -> p (c t)").bitcast(F32)
@@ -131,7 +138,7 @@ def tile_instrumentspecificslotmemory_pa_t_kernel(tc, H, Wr_words, Wr_scales, br
             nc.vector.quantize_mx(
                 out=h_codes[seq][:, part, features].bitcast(FP8X4),
                 scales=h_scales[seq][:, part, features],
-                in_=h_grouped[k][:].rearrange("p h d j -> p (h d) j")[:, features, :].rearrange("p d j -> p (d j)"),
+                in_=h_grouped[k][:, features, :].rearrange("p d j -> p (d j)"),
             )
 
         def quantise_ht(k):
@@ -220,48 +227,71 @@ def tile_instrumentspecificslotmemory_pa_t_kernel(tc, H, Wr_words, Wr_scales, br
             return 0 <= i < N_CHUNKS
 
         last = N_CHUNKS - 1
-        quarter = FEATURES // 4
-        scalar_quarters = (1, last)
+        all_features = slice(0, FEATURES)
+        first_half, last_half = FEATURE_HALVES
+        third_quarter, last_quarter = (slice(q * FEATURES // 4, (q + 1) * FEATURES // 4) for q in (2, 3))
+        vector_copy, scalar_copy = nc.vector.tensor_copy, nc.scalar.copy
 
-        pieces = []
-        for k in range(N_CHUNKS - 1):
-            pieces.append((regroup, nc.vector.tensor_copy, k, 0))
-            pieces.append((regroup, nc.vector.tensor_copy, k, 1, 0, quarter if k in scalar_quarters else 2 * quarter))
-            pieces.append((quantise_h, k, slice(0, FEATURES)))
-        last_features = [FEATURE_HALVES[0], slice(3 * quarter, FEATURES), slice(2 * quarter, 3 * quarter)]
-        pieces += [
-            (regroup, nc.vector.tensor_copy, last, 0),
-            (quantise_h, last, last_features[0]),
-            (regroup, nc.vector.tensor_copy, last, 1, 0, quarter),
-            (quantise_h, last, last_features[1]),
-            (quantise_h, last, last_features[2]),
-        ]
-        pieces_in_step = [3, 1, 2, 2] + [3] * (N_CHUNKS - 5) + [1, 2, 2, len(pieces)]
+        def prepare_h(k):
+            if k == 0:
+                regroup(vector_copy, 0, first_half)
+                regroup(vector_copy, 0, last_half)
+                quantise_h(0, all_features)
+            elif k == 1:
+                regroup(vector_copy, 1, first_half)
+                regroup(vector_copy, 1, third_quarter)
+            elif k == 2:
+                quantise_h(1, all_features)
+                regroup(vector_copy, 2, first_half)
+            elif k == 3:
+                regroup(vector_copy, 2, last_half)
+                quantise_h(2, all_features)
+            elif k < last:
+                if k > 4:
+                    quantise_h(k - 2, all_features)
+                regroup(vector_copy, k - 1, all_features)
+            elif k == last:
+                quantise_h(last - 2, all_features)
+                regroup(vector_copy, last - 1, first_half)
+            elif k == last + 1:
+                regroup(vector_copy, last - 1, last_half)
+                regroup(vector_copy, last, first_half)
+                quantise_h(last - 1, all_features)
+            elif k == last + 2:
+                quantise_h(last, first_half)
+                regroup(vector_copy, last, third_quarter)
+            elif k == last + 3:
+                regroup(vector_copy, last, last_quarter)
+                quantise_h(last, third_quarter)
+                quantise_h(last, last_quarter)
 
-        for k in range(N_CHUNKS + 4):
+        def first_matmul(k):
+            route_logits(k)
+            sigmoid(k)
+
+        for k in range(N_CHUNKS + AGG_LAG):
             if is_chunk(k + PREFETCH):
                 load(k + PREFETCH)
             if is_chunk(k - 1):
                 quantise_ht(k - 1)
             if is_chunk(k - 3):
                 quantise_route(k - 3)
-            if k < len(pieces_in_step):
-                for piece, *where in pieces[: pieces_in_step[k]]:
-                    piece(*where)
-                pieces = pieces[pieces_in_step[k] :]
+            prepare_h(k)
+            t = k - AGG_LAG
             if is_chunk(k):
                 transpose(k)
+            if k == 1:
+                regroup(scalar_copy, 1, last_quarter)
             if is_chunk(k - 2):
                 transpose_route(k - 2)
-            if k == 1 or k == last + 1:
-                regroup(nc.scalar.copy, min(k, last), 1, quarter, 2 * quarter)
-            if is_chunk(k - 1):
-                route_logits(k - 1)
-                sigmoid(k - 1)
-            if is_chunk(k - 4) and k - 4 < N_OUT_TILES - 2:
+            if is_chunk(k - 1) and k - 1 < last:
+                first_matmul(k - 1)
+            if 0 <= t < N_OUT_TILES - 2:
                 for features in FEATURE_HALVES:
-                    aggregate(k - 4, features, nc.scalar.copy)
-            if k - 4 == N_OUT_TILES - 1:
-                for i, features in enumerate(last_features):
-                    aggregate(k - 5, features, nc.scalar.copy if i == 0 else nc.vector.tensor_copy)
-                    aggregate(k - 4, features, nc.scalar.copy)
+                    aggregate(t, features, scalar_copy)
+            if k == last + 1:
+                first_matmul(last)
+            if t == N_OUT_TILES - 1:
+                for i, features in enumerate((first_half, third_quarter, last_quarter)):
+                    aggregate(t - 1, features, scalar_copy if i == 0 else vector_copy)
+                    aggregate(t, features, scalar_copy)

from contextlib import ExitStack
from itertools import product

import concourse.mybir as mybir
from concourse.masks import make_identity

F32 = mybir.dt.float32
BF16 = mybir.dt.bfloat16
I32 = mybir.dt.int32
U32 = mybir.dt.uint32
U8 = mybir.dt.uint8
FP8X4 = mybir.dt.float8_e4m3fn_x4
SIGMOID = mybir.ActivationFunctionType.Sigmoid

SEQS, FRAMES, FEATURES, SLOTS = 8, 1024, 1024, 256

P = 128
PACK = 4
K_PASS = P * PACK
BANK = 512

CHUNK = K_PASS
CHUNKS_PER_SEQ = FRAMES // CHUNK
N_CHUNKS = SEQS * CHUNKS_PER_SEQ
FEATURE_PASSES = FEATURES // K_PASS
WORDS_PER_PASS = K_PASS // 2
SLOT_TILES = SLOTS // P
FEATURE_BANKS = FEATURES // BANK
N_OUT_TILES = SEQS * SLOT_TILES
assert N_OUT_TILES == N_CHUNKS

FEATURE_HALVES = (slice(0, FEATURES // 2), slice(FEATURES // 2, FEATURES))

PREFETCH = 4

AGG_LAG = 5

FLOPS = 2 * 2 * SEQS * FRAMES * FEATURES * SLOTS


def tile_instrumentspecificslotmemory_pa_t_kernel(tc, H, Wr_words, Wr_scales, br, out):
    nc = tc.nc
    with ExitStack() as stack:
        const = stack.enter_context(tc.tile_pool(name="const", bufs=1))
        rows_pool = stack.enter_context(tc.tile_pool(name="rows", bufs=PREFETCH + 4))
        first_pool = stack.enter_context(tc.tile_pool(name="first", bufs=2))
        work = stack.enter_context(tc.tile_pool(name="work", bufs=3))
        seq_pool = stack.enter_context(tc.tile_pool(name="seq", bufs=3))
        grouped_pool = stack.enter_context(tc.tile_pool(name="grouped", bufs=3))
        out_pool = stack.enter_context(tc.tile_pool(name="out", bufs=8))
        psum = stack.enter_context(tc.psum_pool(name="psum", bufs=8))
        stack.enter_context(tc.manual_schedule())

        h_rows, h_grouped, ht_grouped, ht_codes, ht_scales, route_t, route_grouped = {}, {}, {}, {}, {}, {}, {}
        h_codes, h_scales, route_codes, route_scales = {}, {}, {}, {}
        logit_banks = {}

        def load(k):
            seq, part = divmod(k, CHUNKS_PER_SEQ)
            frames = H[seq, part * CHUNK : (part + 1) * CHUNK, :].rearrange("(p j) d -> p j d", j=PACK)
            if k < 2:
                rows = first_pool.tile([P, 2, PACK, FEATURES // 2], BF16)
                for half, j in product(range(2), (0, PACK // 2)):
                    nc.sync.dma_start(
                        out=rows[:, half, j : j + 2, :], in_=frames[:, j : j + 2, FEATURE_HALVES[half]]
                    )
            else:
                rows = rows_pool.tile([P, PACK, FEATURES], BF16)
                nc.sync.dma_start(out=rows[:], in_=frames)
            h_rows[k] = rows

        def rows_of(k, features):
            if k < 2:
                half, start = divmod(features.start, FEATURES // 2)
                return h_rows[k][:, half, :, start : start + features.stop - features.start]
            return h_rows[k][:, :, features]

        load(0)
        load(1)

        w_words = const.tile([P, FEATURE_PASSES, SLOTS], U32, align_bytes=64)
        nc.sync.dma_start(
            out=w_words[:].bitcast(I32),
            in_=Wr_words.rearrange("g p n t -> p g (n t)").bitcast(I32),
        )
        w_scales = const.tile([P, FEATURE_PASSES, SLOTS], U8, align_bytes=64)
        nc.vector.memset(w_scales[:].bitcast(I32), 0)
        for quadrant in range(4):
            nc.sync.dma_start(
                out=w_scales[32 * quadrant : 32 * quadrant + 4, :, :].bitcast(I32),
                in_=Wr_scales[:, 4 * quadrant : 4 * quadrant + 4, :].rearrange("g r n -> r g n").bitcast(I32),
            )
        identity = const.tile([P, P], F32)
        make_identity(nc, identity[:])

        bias = const.tile([P, SLOT_TILES, 16], BF16)
        with nc.allow_non_contiguous_dma(reason="256 bias values, one to a partition"):
            for s in range(SLOT_TILES):
                nc.scalar.dma_start(out=bias[:, s, 0:1], in_=br[s * P : (s + 1) * P].unsqueeze(1))
        for k in range(2, PREFETCH):
            load(k)

        warm_in = const.tile([P, 1], F32)
        warm_out = const.tile([P, 1], F32)
        nc.vector.memset(warm_in[:], 0.0)
        nc.scalar.activation(out=warm_out[:], in_=warm_in[:], func=SIGMOID)

        def regroup(copy, k, features):
            if k not in h_grouped:
                h_grouped[k] = grouped_pool.tile([P, FEATURES, PACK], BF16, align_bytes=64, name="h_grouped")
            copy(
                out=h_grouped[k][:, features, :].rearrange("p (c i) j -> p c j i", i=4),
                in_=rows_of(k, features).rearrange("p j (c i) -> p c j i", i=4),
            )

        def transpose(k):
            ht_grouped[k] = work.tile([P, FEATURE_PASSES, CHUNK, PACK], BF16, align_bytes=64, name="ht_grouped")
            for g, half in product(range(FEATURE_PASSES), range(2)):
                bank = psum.tile([P, 2, 2, P], F32, name="ht_bank", tag="bank")
                for jj in range(2):
                    for u in range(2):
                        nc.tensor.transpose(
                            bank[:, u, jj, :],
                            rows_of(k, FEATURE_HALVES[g]).bitcast(F32)[:, 2 * half + jj, u:WORDS_PER_PASS:2],
                            identity[:],
                        )
                grouped_words = ht_grouped[k][:, g, :, :].rearrange("p c t -> p (c t)").bitcast(F32)
                nc.scalar.copy(
                    out=grouped_words[:, half * BANK : (half + 1) * BANK].rearrange("p (c u) -> p c u", u=2),
                    in_=bank[:].rearrange("p u j c -> p (j c) u"),
                )

        def quantise_h(k, features):
            seq, part = divmod(k, CHUNKS_PER_SEQ)
            if part == 0 and features.start == 0:
                h_codes[seq] = seq_pool.tile([P, CHUNKS_PER_SEQ, FEATURES], U32, align_bytes=64, name="h_codes")
                h_scales[seq] = seq_pool.tile([P, CHUNKS_PER_SEQ, FEATURES], U8, align_bytes=64, name="h_scales")
            nc.vector.quantize_mx(
                out=h_codes[seq][:, part, features].bitcast(FP8X4),
                scales=h_scales[seq][:, part, features],
                in_=h_grouped[k][:, features, :].rearrange("p d j -> p (d j)"),
            )

        def quantise_ht(k):
            codes = work.tile([P, FEATURE_PASSES, CHUNK], U32, align_bytes=64, name="ht_codes")
            scales = work.tile([P, FEATURE_PASSES, CHUNK], U8, align_bytes=64, name="ht_scales")
            nc.vector.quantize_mx(
                out=codes[:].rearrange("p g c -> p (g c)").bitcast(FP8X4),
                scales=scales[:].rearrange("p g c -> p (g c)"),
                in_=ht_grouped[k][:].rearrange("p g c t -> p (g c t)"),
            )
            ht_codes[k], ht_scales[k] = codes, scales

        def route_logits(k):
            codes, scales = ht_codes[k], ht_scales[k]
            logit_banks[k] = []
            for s in range(SLOT_TILES):
                slots = slice(s * P, (s + 1) * P)
                bank = psum.tile([P, CHUNK], F32, name="logit_bank", tag="bank")
                for g in range(FEATURE_PASSES):
                    nc.tensor.matmul_mx(
                        out=bank[:],
                        lhsT=w_words[:, g, slots].bitcast(FP8X4),
                        lhsT_scale=w_scales[:, g, slots],
                        rhs=codes[:, g, :].bitcast(FP8X4),
                        rhs_scale=scales[:, g, :],
                        start=(g == 0),
                        stop=(g == FEATURE_PASSES - 1),
                    )
                logit_banks[k].append(bank)

        def sigmoid(k):
            route_t[k] = work.tile([P, SLOT_TILES, CHUNK], BF16, align_bytes=64, name="route_t")
            for s, bank in enumerate(logit_banks[k]):
                nc.scalar.activation(
                    out=route_t[k][:, s, :].rearrange("p (u c e) -> p u c e", u=2, e=2),
                    in_=bank[:].rearrange("p (u e c) -> p u c e", u=2, e=2),
                    func=SIGMOID,
                    bias=bias[:, s, 0:1],
                )

        def transpose_route(k):
            words = route_t[k][:].bitcast(F32)
            bank = psum.tile([P, 2, SLOTS], F32, name="route_bank", tag="bank")
            for s in range(SLOT_TILES):
                for u in range(2):
                    nc.tensor.transpose(
                        bank[:, u, s * P : (s + 1) * P], words[:, s, u * P : (u + 1) * P], identity[:]
                    )
            route_grouped[k] = work.tile([P, SLOTS, PACK], BF16, align_bytes=64, name="route_grouped")
            nc.scalar.copy(
                out=route_grouped[k][:].rearrange("p n j -> p (n j)").bitcast(F32).rearrange("p (n u) -> p n u", u=2),
                in_=bank[:].rearrange("p u n -> p n u"),
            )

        def quantise_route(k):
            seq, part = divmod(k, CHUNKS_PER_SEQ)
            if part == 0:
                route_codes[seq] = seq_pool.tile([P, CHUNKS_PER_SEQ, SLOTS], U32, align_bytes=64, name="route_codes")
                route_scales[seq] = seq_pool.tile([P, CHUNKS_PER_SEQ, SLOTS], U8, align_bytes=64, name="route_scales")
            nc.vector.quantize_mx(
                out=route_codes[seq][:, part, :].bitcast(FP8X4),
                scales=route_scales[seq][:, part, :],
                in_=route_grouped[k][:].rearrange("p n j -> p (n j)"),
            )

        def aggregate(t, features, copy):
            seq, s = divmod(t, SLOT_TILES)
            slots = slice(s * P, (s + 1) * P)
            width = features.stop - features.start
            bank = psum.tile([P, width], F32, name="agg_bank", tag="bank")
            for part in range(CHUNKS_PER_SEQ):
                nc.tensor.matmul_mx(
                    out=bank[:],
                    lhsT=route_codes[seq][:, part, slots].bitcast(FP8X4),
                    lhsT_scale=route_scales[seq][:, part, slots],
                    rhs=h_codes[seq][:, part, features].bitcast(FP8X4),
                    rhs_scale=h_scales[seq][:, part, features],
                    start=(part == 0),
                    stop=(part == CHUNKS_PER_SEQ - 1),
                )
            result = out_pool.tile([P, width], F32)
            copy(out=result[:], in_=bank[:])
            nc.sync.dma_start(out=out[seq, s * P : (s + 1) * P, features], in_=result[:])

        def is_chunk(i):
            return 0 <= i < N_CHUNKS

        last = N_CHUNKS - 1
        all_features = slice(0, FEATURES)
        first_half, last_half = FEATURE_HALVES
        third_quarter, last_quarter = (slice(q * FEATURES // 4, (q + 1) * FEATURES // 4) for q in (2, 3))
        vector_copy, scalar_copy = nc.vector.tensor_copy, nc.scalar.copy

        def prepare_h(k):
            if k == 0:
                regroup(vector_copy, 0, first_half)
                regroup(vector_copy, 0, last_half)
                quantise_h(0, all_features)
            elif k == 1:
                regroup(vector_copy, 1, first_half)
                regroup(vector_copy, 1, third_quarter)
            elif k == 2:
                quantise_h(1, all_features)
                regroup(vector_copy, 2, first_half)
            elif k == 3:
                regroup(vector_copy, 2, last_half)
                quantise_h(2, all_features)
            elif k < last:
                if k > 4:
                    quantise_h(k - 2, all_features)
                regroup(vector_copy, k - 1, all_features)
            elif k == last:
                quantise_h(last - 2, all_features)
                regroup(vector_copy, last - 1, first_half)
            elif k == last + 1:
                regroup(vector_copy, last - 1, last_half)
                regroup(vector_copy, last, first_half)
                quantise_h(last - 1, all_features)
            elif k == last + 2:
                quantise_h(last, first_half)
                regroup(vector_copy, last, third_quarter)
            elif k == last + 3:
                regroup(vector_copy, last, last_quarter)
                quantise_h(last, third_quarter)
                quantise_h(last, last_quarter)

        def first_matmul(k):
            route_logits(k)
            sigmoid(k)

        for k in range(N_CHUNKS + AGG_LAG):
            if is_chunk(k + PREFETCH):
                load(k + PREFETCH)
            if is_chunk(k - 1):
                quantise_ht(k - 1)
            if is_chunk(k - 3):
                quantise_route(k - 3)
            prepare_h(k)
            t = k - AGG_LAG
            if is_chunk(k):
                transpose(k)
            if k == 1:
                regroup(scalar_copy, 1, last_quarter)
            if is_chunk(k - 2):
                transpose_route(k - 2)
            if is_chunk(k - 1) and k - 1 < last:
                first_matmul(k - 1)
            if 0 <= t < N_OUT_TILES - 2:
                for features in FEATURE_HALVES:
                    aggregate(t, features, scalar_copy)
            if k == last + 1:
                first_matmul(last)
            if t == N_OUT_TILES - 1:
                for i, features in enumerate((first_half, third_quarter, last_quarter)):
                    aggregate(t - 1, features, scalar_copy if i == 0 else vector_copy)
                    aggregate(t, features, scalar_copy)
